import numpy as np
import ml_dtypes


def mxq(x, axis, fmt="e4m3"):
    dtype, down = {"e4m3": (ml_dtypes.float8_e4m3fn, 7), "e5m2": (ml_dtypes.float8_e5m2, 14)}[fmt]
    v = np.moveaxis(np.asarray(x, np.float32).astype(ml_dtypes.bfloat16).astype(np.float64), axis, -1)
    blocks = v.reshape(v.shape[:-1] + (-1, 32))
    amax = np.abs(blocks).max(-1, keepdims=True)
    byte = np.maximum(np.where(amax > 0, np.frexp(amax)[1] - 1 + 127, 0) - down, 1)
    scale = np.exp2(byte - 127.0)
    codes = (blocks / scale).astype(np.float32).astype(dtype).astype(np.float64)
    return np.moveaxis((codes * scale).reshape(v.shape), -1, axis)


WIDE = False


def mx_kscale(k):
    if not WIDE:
        return np.ones(k)
    levels = np.array([10, -10, 5, -5, 0])
    a = np.random.permutation(np.resize(levels, k // 512 * 4)).reshape(k // 512, 4)
    idx = np.arange(k)
    return np.exp2(a[idx // 512, idx % 128 // 32])


BF16 = ml_dtypes.bfloat16


def bf(x):
    return np.asarray(x, np.float32).astype(BF16)


def f64(x):
    return np.asarray(x).astype(np.float64)


B, T, N, C, WIN, F = 2, 5, 512, 1024, 2, 3
NW = T - WIN + 1
K = WIN * N


def setup_inputs():
    s = mx_kscale(N)
    return {"data_temb": bf(np.random.standard_normal((B, T, N, C)) * s[:, None]),
            "adj_mid": bf(np.random.standard_normal((N, K)) / np.sqrt(K) / np.tile(s, WIN)),
            "spatial_emb": bf(np.random.standard_normal((1, 1, N, C)) * 0.3 * s[:, None])}


def reference(data_temb, adj_mid, spatial_emb):
    x = f64(data_temb) + f64(spatial_emb)
    xq = mxq(x, 2, "e4m3")
    idx = np.arange(NW)[:, None] + np.arange(WIN)[None, :]
    return mxq(f64(adj_mid), 1, "e4m3") @ xq[:, idx].reshape(B, NW, K, C)

@@ -1,0 +1,142 @@
+from contextlib import ExitStack
+
+import concourse.mybir as mybir
+from concourse.masks import make_identity
+
+F32 = mybir.dt.float32
+BF16 = mybir.dt.bfloat16
+U32 = mybir.dt.uint32
+U8 = mybir.dt.uint8
+FP8X4 = mybir.dt.float8_e4m3fn_x4
+
+B, T, NODES, C, WIN = 2, 5, 512, 1024, 2
+NW = T - WIN + 1
+P = 128
+PACK = 4
+N_TILE = 512
+HALVES = C // N_TILE
+M_TILES = NODES // P
+FLOPS = 2 * B * NW * NODES * (WIN * NODES) * C
+
+
+def tile_stsindividuallayer_pa_t_kernel(tc, data_temb, adj_mid, spatial_emb, out):
+    nc = tc.nc
+    with ExitStack() as ctx:
+        const = ctx.enter_context(tc.tile_pool(name="const", bufs=1))
+        raw_pool = ctx.enter_context(tc.tile_pool(name="raw", bufs=B * T))
+        grouped_pool = ctx.enter_context(tc.tile_pool(name="grouped", bufs=3))
+        mx_pool = ctx.enter_context(tc.tile_pool(name="mx", bufs=4))
+        stage_pool = ctx.enter_context(tc.tile_pool(name="stage", bufs=6))
+        psum = ctx.enter_context(tc.psum_pool(name="psum", bufs=8))
+        ctx.enter_context(tc.manual_schedule())
+
+        steps = [(b, t) for b in range(B) for t in range(T)]
+        sp_raw = const.tile([P, PACK, C], BF16)
+        adj_raw = const.tile([P, M_TILES, WIN * NODES], BF16)
+        raw = {}
+        for bt in steps:
+            raw[bt] = raw_pool.tile([P, PACK, C], BF16, name="raw")
+
+        def load_step(bt):
+            nc.sync.dma_start(
+                out=raw[bt][:], in_=data_temb[bt[0], bt[1]].rearrange("(p j) c -> p j c", j=PACK)
+            )
+
+        nc.sync.dma_start(out=sp_raw[:], in_=spatial_emb[0, 0].rearrange("(p j) c -> p j c", j=PACK))
+        load_step(steps[0])
+        nc.sync.dma_start(out=adj_raw[:], in_=adj_mid.rearrange("(p i) k -> p i k", i=M_TILES))
+        for bt in steps[1:]:
+            load_step(bt)
+
+        ident = const.tile([P, P], F32)
+        make_identity(nc, ident[:])
+
+        sp_grouped = const.tile([P, C, PACK], BF16)
+        nc.vector.tensor_copy(
+            out=sp_grouped[:, 0:N_TILE, :], in_=sp_raw[:, :, 0:N_TILE].rearrange("p j c -> p c j")
+        )
+        nc.scalar.copy(
+            out=sp_grouped[:, N_TILE:C, :], in_=sp_raw[:, :, N_TILE:C].rearrange("p j c -> p c j")
+        )
+
+        adj_words = adj_raw[:].bitcast(F32).rearrange("p i (g q u) -> p i g q u", g=WIN, u=2)
+        adj_grouped = const.tile([P, WIN, M_TILES * P * PACK], BF16, align_bytes=64)
+        adj_grouped_words = adj_grouped[:].bitcast(F32).rearrange(
+            "p g (i m u) -> p g i m u", i=M_TILES, u=2
+        )
+        adj_codes = const.tile([P, WIN, NODES], U32, align_bytes=64)
+        adj_scales = const.tile([P, WIN, NODES], U8, align_bytes=64)
+        for g in range(WIN):
+            for i0 in range(0, M_TILES, 2):
+                turned = psum.tile([P, 2, 2, P], F32, tag="bank")
+                for i in range(2):
+                    for u in range(2):
+                        nc.tensor.transpose(turned[:, i, u, :], adj_words[:, i0 + i, g, :, u], ident[:])
+                nc.scalar.copy(
+                    out=adj_grouped_words[:, g, i0 : i0 + 2, :, :],
+                    in_=turned[:].rearrange("p i u m -> p i m u"),
+                )
+
+        def quantise_adj():
+            for g in range(WIN):
+                nc.vector.quantize_mx(
+                    out=adj_codes[:, g, :].bitcast(FP8X4), scales=adj_scales[:, g, :], in_=adj_grouped[:, g, :]
+                )
+
+        grouped, codes, scales, stage = {}, {}, {}, {}
+
+        def add_spatial(b, t, h):
+            if h == 0:
+                grouped[(b, t)] = grouped_pool.tile([P, C, PACK], BF16, name="grouped", align_bytes=64)
+            cols = slice(h * N_TILE, (h + 1) * N_TILE)
+            nc.vector.tensor_tensor(
+                out=grouped[(b, t)][:, cols, :],
+                in0=raw[(b, t)][:, :, cols].rearrange("p j c -> p c j"),
+                in1=sp_grouped[:, cols, :],
+                op=mybir.AluOpType.add,
+            )
+
+        def quantise(b, t, h):
+            if h == 0:
+                codes[(b, t)] = mx_pool.tile([P, C], U32, name="codes", align_bytes=64)
+                scales[(b, t)] = mx_pool.tile([P, C], U8, name="scales", align_bytes=64)
+            cols = slice(h * N_TILE, (h + 1) * N_TILE)
+            nc.vector.quantize_mx(
+                out=codes[(b, t)][:, cols].bitcast(FP8X4),
+                scales=scales[(b, t)][:, cols],
+                in_=grouped[(b, t)][:, cols, :].rearrange("p c j -> p (c j)"),
+            )
+
+        def aggregate(b, t, h):
+            if t == 0:
+                return
+            w = t - 1
+            cols = slice(h * N_TILE, (h + 1) * N_TILE)
+            out_rows = out[b, w].rearrange("(p i) c -> p i c", i=M_TILES)
+            for i in range(M_TILES):
+                if h == 0 and i % 2 == 0:
+                    stage[i // 2] = stage_pool.tile([P, 2, C], F32, name="stage")
+                acc = psum.tile([P, N_TILE], F32, tag="bank")
+                for g in range(WIN):
+                    nc.tensor.matmul_mx(
+                        out=acc[:],
+                        lhsT=adj_codes[:, g, i * P : (i + 1) * P].bitcast(FP8X4),
+                        lhsT_scale=adj_scales[:, g, i * P : (i + 1) * P],
+                        rhs=codes[(b, w + g)][:, cols].bitcast(FP8X4),
+                        rhs_scale=scales[(b, w + g)][:, cols],
+                        start=(g == 0),
+                        stop=(g == WIN - 1),
+                    )
+                nc.scalar.copy(out=stage[i // 2][:, i % 2, cols], in_=acc[:])
+                if h == HALVES - 1 and i % 2 == 1:
+                    nc.sync.dma_start(out=out_rows[:, i - 1 : i + 1, :], in_=stage[i // 2][:])
+
+        chunks = [(b, t, h) for (b, t) in steps for h in range(HALVES)]
+        for n in range(len(chunks) + 1):
+            if n < len(chunks):
+                add_spatial(*chunks[n])
+            if n == 3:
+                quantise_adj()
+            if n >= 1:
+                quantise(*chunks[n - 1])
+                aggregate(*chunks[n - 1])

@@ -16,6 +16,8 @@ PACK = 4
 N_TILE = 512
 HALVES = C // N_TILE
 M_TILES = NODES // P
+RUN = 4
+ADJ_AT = 3
 FLOPS = 2 * B * NW * NODES * (WIN * NODES) * C
 
 
@@ -51,14 +53,6 @@ def tile_stsindividuallayer_pa_t_kernel(tc, data_temb, adj_mid, spatial_emb, out
         ident = const.tile([P, P], F32)
         make_identity(nc, ident[:])
 
-        sp_grouped = const.tile([P, C, PACK], BF16)
-        nc.vector.tensor_copy(
-            out=sp_grouped[:, 0:N_TILE, :], in_=sp_raw[:, :, 0:N_TILE].rearrange("p j c -> p c j")
-        )
-        nc.scalar.copy(
-            out=sp_grouped[:, N_TILE:C, :], in_=sp_raw[:, :, N_TILE:C].rearrange("p j c -> p c j")
-        )
-
         adj_words = adj_raw[:].bitcast(F32).rearrange("p i (g q u) -> p i g q u", g=WIN, u=2)
         adj_grouped = const.tile([P, WIN, M_TILES * P * PACK], BF16, align_bytes=64)
         adj_grouped_words = adj_grouped[:].bitcast(F32).rearrange(
@@ -86,14 +80,21 @@ def tile_stsindividuallayer_pa_t_kernel(tc, data_temb, adj_mid, spatial_emb, out
         grouped, codes, scales, stage = {}, {}, {}, {}
 
         def add_spatial(b, t, h):
+            cols = slice(h * N_TILE, (h + 1) * N_TILE)
+            nc.vector.tensor_tensor(
+                out=raw[(b, t)][:, :, cols],
+                in0=raw[(b, t)][:, :, cols],
+                in1=sp_raw[:, :, cols],
+                op=mybir.AluOpType.add,
+            )
+
+        def regroup(b, t, h):
             if h == 0:
                 grouped[(b, t)] = grouped_pool.tile([P, C, PACK], BF16, name="grouped", align_bytes=64)
             cols = slice(h * N_TILE, (h + 1) * N_TILE)
-            nc.vector.tensor_tensor(
-                out=grouped[(b, t)][:, cols, :],
-                in0=raw[(b, t)][:, :, cols].rearrange("p j c -> p c j"),
-                in1=sp_grouped[:, cols, :],
-                op=mybir.AluOpType.add,
+            nc.vector.tensor_copy(
+                out=grouped[(b, t)][:, cols, :].rearrange("p (c r) j -> p c j r", r=RUN),
+                in_=raw[(b, t)][:, :, cols].rearrange("p j (c r) -> p c j r", r=RUN),
             )
 
         def quantise(b, t, h):
@@ -132,11 +133,13 @@ def tile_stsindividuallayer_pa_t_kernel(tc, data_temb, adj_mid, spatial_emb, out
                     nc.sync.dma_start(out=out_rows[:, i - 1 : i + 1, :], in_=stage[i // 2][:])
 
         chunks = [(b, t, h) for (b, t) in steps for h in range(HALVES)]
-        for n in range(len(chunks) + 1):
+        for n in range(len(chunks) + 2):
             if n < len(chunks):
                 add_spatial(*chunks[n])
-            if n == 3:
+            if n == ADJ_AT:
                 quantise_adj()
-            if n >= 1:
-                quantise(*chunks[n - 1])
-                aggregate(*chunks[n - 1])
+            if n >= 2:
+                quantise(*chunks[n - 2])
+                aggregate(*chunks[n - 2])
+            if 1 <= n <= len(chunks):
+                regroup(*chunks[n - 1])

@@ -17,7 +17,10 @@ N_TILE = 512
 HALVES = C // N_TILE
 M_TILES = NODES // P
 RUN = 4
-ADJ_AT = 3
+SCALAR_COLS_EARLY = 384
+EARLY_CHUNKS = 6
+SCALAR_COLS_BUSY = 64
+ADJ_AT = 4
 FLOPS = 2 * B * NW * NODES * (WIN * NODES) * C
 
 
@@ -27,12 +30,12 @@ def tile_stsindividuallayer_pa_t_kernel(tc, data_temb, adj_mid, spatial_emb, out
         const = ctx.enter_context(tc.tile_pool(name="const", bufs=1))
         raw_pool = ctx.enter_context(tc.tile_pool(name="raw", bufs=B * T))
         grouped_pool = ctx.enter_context(tc.tile_pool(name="grouped", bufs=3))
-        mx_pool = ctx.enter_context(tc.tile_pool(name="mx", bufs=4))
-        stage_pool = ctx.enter_context(tc.tile_pool(name="stage", bufs=6))
+        mx_pool = ctx.enter_context(tc.tile_pool(name="mx", bufs=6))
+        stage_pool = ctx.enter_context(tc.tile_pool(name="stage", bufs=8))
         psum = ctx.enter_context(tc.psum_pool(name="psum", bufs=8))
         ctx.enter_context(tc.manual_schedule())
 
-        steps = [(b, t) for b in range(B) for t in range(T)]
+        steps = [(b, t) for t in range(T) for b in range(B)]
         sp_raw = const.tile([P, PACK, C], BF16)
         adj_raw = const.tile([P, M_TILES, WIN * NODES], BF16)
         raw = {}
@@ -44,10 +47,15 @@ def tile_stsindividuallayer_pa_t_kernel(tc, data_temb, adj_mid, spatial_emb, out
                 out=raw[bt][:], in_=data_temb[bt[0], bt[1]].rearrange("(p j) c -> p j c", j=PACK)
             )
 
-        nc.sync.dma_start(out=sp_raw[:], in_=spatial_emb[0, 0].rearrange("(p j) c -> p j c", j=PACK))
-        load_step(steps[0])
+        for h in range(HALVES):
+            cols = slice(h * N_TILE, (h + 1) * N_TILE)
+            for tile_, rows in ((sp_raw, spatial_emb[0, 0]), (raw[steps[0]], data_temb[steps[0][0], steps[0][1]])):
+                nc.sync.dma_start(
+                    out=tile_[:, :, cols], in_=rows.rearrange("(p j) c -> p j c", j=PACK)[:, :, cols]
+                )
+        load_step(steps[1])
         nc.sync.dma_start(out=adj_raw[:], in_=adj_mid.rearrange("(p i) k -> p i k", i=M_TILES))
-        for bt in steps[1:]:
+        for bt in steps[2:]:
             load_step(bt)
 
         ident = const.tile([P, P], F32)
@@ -60,16 +68,18 @@ def tile_stsindividuallayer_pa_t_kernel(tc, data_temb, adj_mid, spatial_emb, out
         )
         adj_codes = const.tile([P, WIN, NODES], U32, align_bytes=64)
         adj_scales = const.tile([P, WIN, NODES], U8, align_bytes=64)
-        for g in range(WIN):
-            for i0 in range(0, M_TILES, 2):
-                turned = psum.tile([P, 2, 2, P], F32, tag="bank")
-                for i in range(2):
-                    for u in range(2):
-                        nc.tensor.transpose(turned[:, i, u, :], adj_words[:, i0 + i, g, :, u], ident[:])
-                nc.scalar.copy(
-                    out=adj_grouped_words[:, g, i0 : i0 + 2, :, :],
-                    in_=turned[:].rearrange("p i u m -> p i m u"),
-                )
+
+        def turn_adj():
+            for g in range(WIN):
+                for i0 in range(0, M_TILES, 2):
+                    turned = psum.tile([P, 2, 2, P], F32, tag="bank")
+                    for i in range(2):
+                        for u in range(2):
+                            nc.tensor.transpose(turned[:, i, u, :], adj_words[:, i0 + i, g, :, u], ident[:])
+                    nc.scalar.copy(
+                        out=adj_grouped_words[:, g, i0 : i0 + 2, :, :],
+                        in_=turned[:].rearrange("p i u m -> p i m u"),
+                    )
 
         def quantise_adj():
             for g in range(WIN):
@@ -88,14 +98,23 @@ def tile_stsindividuallayer_pa_t_kernel(tc, data_temb, adj_mid, spatial_emb, out
                 op=mybir.AluOpType.add,
             )
 
-        def regroup(b, t, h):
-            if h == 0:
-                grouped[(b, t)] = grouped_pool.tile([P, C, PACK], BF16, name="grouped", align_bytes=64)
-            cols = slice(h * N_TILE, (h + 1) * N_TILE)
-            nc.vector.tensor_copy(
+        def regroup(copy, b, t, cols):
+            copy(
                 out=grouped[(b, t)][:, cols, :].rearrange("p (c r) j -> p c j r", r=RUN),
                 in_=raw[(b, t)][:, :, cols].rearrange("p j (c r) -> p c j r", r=RUN),
             )
+
+        def scalar_split(b, t, h):
+            early = chunks.index((b, t, h)) < EARLY_CHUNKS
+            return (h + 1) * N_TILE - (SCALAR_COLS_EARLY if early else SCALAR_COLS_BUSY)
+
+        def regroup_on_scalar(b, t, h):
+            if h == 0:
+                grouped[(b, t)] = grouped_pool.tile([P, C, PACK], BF16, name="grouped", align_bytes=64)
+            regroup(nc.scalar.copy, b, t, slice(scalar_split(b, t, h), (h + 1) * N_TILE))
+
+        def regroup_on_vector(b, t, h):
+            regroup(nc.vector.tensor_copy, b, t, slice(h * N_TILE, scalar_split(b, t, h)))
 
         def quantise(b, t, h):
             if h == 0:
@@ -114,13 +133,13 @@ def tile_stsindividuallayer_pa_t_kernel(tc, data_temb, adj_mid, spatial_emb, out
             w = t - 1
             cols = slice(h * N_TILE, (h + 1) * N_TILE)
             out_rows = out[b, w].rearrange("(p i) c -> p i c", i=M_TILES)
-            for i in range(M_TILES):
-                if h == 0 and i % 2 == 0:
-                    stage[i // 2] = stage_pool.tile([P, 2, C], F32, name="stage")
-                acc = psum.tile([P, N_TILE], F32, tag="bank")
-                for g in range(WIN):
+            acc = {}
+            for g in range(WIN):
+                for i in range(M_TILES):
+                    if g == 0:
+                        acc[i] = psum.tile([P, N_TILE], F32, name="acc", tag="bank")
                     nc.tensor.matmul_mx(
-                        out=acc[:],
+                        out=acc[i][:],
                         lhsT=adj_codes[:, g, i * P : (i + 1) * P].bitcast(FP8X4),
                         lhsT_scale=adj_scales[:, g, i * P : (i + 1) * P],
                         rhs=codes[(b, w + g)][:, cols].bitcast(FP8X4),
@@ -128,18 +147,29 @@ def tile_stsindividuallayer_pa_t_kernel(tc, data_temb, adj_mid, spatial_emb, out
                         start=(g == 0),
                         stop=(g == WIN - 1),
                     )
-                nc.scalar.copy(out=stage[i // 2][:, i % 2, cols], in_=acc[:])
-                if h == HALVES - 1 and i % 2 == 1:
-                    nc.sync.dma_start(out=out_rows[:, i - 1 : i + 1, :], in_=stage[i // 2][:])
+            by_halves = w == NW - 1
+            last_chunk = (b, t, h) == chunks[-1]
+            for i in range(M_TILES):
+                if h == 0 and i % 2 == 0:
+                    stage[(b, i // 2)] = stage_pool.tile([P, 2, C], F32, name="stage")
+                empty = nc.vector.tensor_copy if last_chunk and i % 2 == 1 else nc.scalar.copy
+                empty(out=stage[(b, i // 2)][:, i % 2, cols], in_=acc[i][:])
+                if i % 2 == 1 and (by_halves or h == HALVES - 1):
+                    stored = cols if by_halves else slice(0, C)
+                    nc.sync.dma_start(out=out_rows[:, i - 1 : i + 1, stored], in_=stage[(b, i // 2)][:, :, stored])
 
         chunks = [(b, t, h) for (b, t) in steps for h in range(HALVES)]
         for n in range(len(chunks) + 2):
             if n < len(chunks):
                 add_spatial(*chunks[n])
+            if 1 <= n <= len(chunks):
+                regroup_on_scalar(*chunks[n - 1])
             if n == ADJ_AT:
+                turn_adj()
+            if n == ADJ_AT + 1:
                 quantise_adj()
             if n >= 2:
                 quantise(*chunks[n - 2])
                 aggregate(*chunks[n - 2])
             if 1 <= n <= len(chunks):
-                regroup(*chunks[n - 1])
+                regroup_on_vector(*chunks[n - 1])

@@ -16,7 +16,7 @@ PACK = 4
 N_TILE = 512
 HALVES = C // N_TILE
 M_TILES = NODES // P
-RUN = 4
+RUN = 8
 SCALAR_COLS_EARLY = 384
 EARLY_CHUNKS = 6
 SCALAR_COLS_BUSY = 64

@@ -14,13 +14,17 @@ NW = T - WIN + 1
 P = 128
 PACK = 4
 N_TILE = 512
-HALVES = C // N_TILE
 M_TILES = NODES // P
 RUN = 8
-SCALAR_COLS_EARLY = 384
-EARLY_CHUNKS = 6
-SCALAR_COLS_BUSY = 64
-ADJ_AT = 4
+FIRST_WIDTHS = (512, 512)
+EARLY_WIDTHS = (512, 512)
+MIDDLE_WIDTHS = (512, 512)
+LAST_WIDTHS = (512, 512)
+EARLY_STEPS = 3
+SCALAR_EARLY = (7, 8)
+SCALAR_BUSY = (3, 16)
+VECTOR_HELPS = 1
+ADJ_AFTER = 2
 FLOPS = 2 * B * NW * NODES * (WIN * NODES) * C
 
 
@@ -36,6 +40,20 @@ def tile_stsindividuallayer_pa_t_kernel(tc, data_temb, adj_mid, spatial_emb, out
         ctx.enter_context(tc.manual_schedule())
 
         steps = [(b, t) for t in range(T) for b in range(B)]
+        pieces = []
+        for s, (b, t) in enumerate(steps):
+            widths = MIDDLE_WIDTHS
+            if s == 0:
+                widths = FIRST_WIDTHS
+            elif s < EARLY_STEPS:
+                widths = EARLY_WIDTHS
+            elif s == len(steps) - 1:
+                widths = LAST_WIDTHS
+            first = 0
+            for width in widths:
+                pieces.append((s, b, t, first, width))
+                first += width
+
         sp_raw = const.tile([P, PACK, C], BF16)
         adj_raw = const.tile([P, M_TILES, WIN * NODES], BF16)
         raw = {}
@@ -47,15 +65,17 @@ def tile_stsindividuallayer_pa_t_kernel(tc, data_temb, adj_mid, spatial_emb, out
                 out=raw[bt][:], in_=data_temb[bt[0], bt[1]].rearrange("(p j) c -> p j c", j=PACK)
             )
 
-        for h in range(HALVES):
-            cols = slice(h * N_TILE, (h + 1) * N_TILE)
-            for tile_, rows in ((sp_raw, spatial_emb[0, 0]), (raw[steps[0]], data_temb[steps[0][0], steps[0][1]])):
-                nc.sync.dma_start(
-                    out=tile_[:, :, cols], in_=rows.rearrange("(p j) c -> p j c", j=PACK)[:, :, cols]
-                )
-        load_step(steps[1])
+        for s, b, t, first, width in pieces:
+            if s == 0:
+                cols = slice(first, first + width)
+                for tile_, rows in ((sp_raw, spatial_emb[0, 0]), (raw[(b, t)], data_temb[b, t])):
+                    nc.sync.dma_start(
+                        out=tile_[:, :, cols], in_=rows.rearrange("(p j) c -> p j c", j=PACK)[:, :, cols]
+                    )
+        for bt in steps[1:ADJ_AFTER]:
+            load_step(bt)
         nc.sync.dma_start(out=adj_raw[:], in_=adj_mid.rearrange("(p i) k -> p i k", i=M_TILES))
-        for bt in steps[2:]:
+        for bt in steps[ADJ_AFTER:]:
             load_step(bt)
 
         ident = const.tile([P, P], F32)
@@ -89,8 +109,8 @@ def tile_stsindividuallayer_pa_t_kernel(tc, data_temb, adj_mid, spatial_emb, out
 
         grouped, codes, scales, stage = {}, {}, {}, {}
 
-        def add_spatial(b, t, h):
-            cols = slice(h * N_TILE, (h + 1) * N_TILE)
+        def add_spatial(s, b, t, first, width):
+            cols = slice(first, first + width)
             nc.vector.tensor_tensor(
                 out=raw[(b, t)][:, :, cols],
                 in0=raw[(b, t)][:, :, cols],
@@ -104,34 +124,34 @@ def tile_stsindividuallayer_pa_t_kernel(tc, data_temb, adj_mid, spatial_emb, out
                 in_=raw[(b, t)][:, :, cols].rearrange("p j (c r) -> p c j r", r=RUN),
             )
 
-        def scalar_split(b, t, h):
-            early = chunks.index((b, t, h)) < EARLY_CHUNKS
-            return (h + 1) * N_TILE - (SCALAR_COLS_EARLY if early else SCALAR_COLS_BUSY)
+        def scalar_split(s, first, width):
+            share = SCALAR_EARLY if s < EARLY_STEPS else SCALAR_BUSY
+            return first + width - width * share[0] // share[1]
 
-        def regroup_on_scalar(b, t, h):
-            if h == 0:
+        def regroup_on_scalar(s, b, t, first, width):
+            if first == 0:
                 grouped[(b, t)] = grouped_pool.tile([P, C, PACK], BF16, name="grouped", align_bytes=64)
-            regroup(nc.scalar.copy, b, t, slice(scalar_split(b, t, h), (h + 1) * N_TILE))
+            regroup(nc.scalar.copy, b, t, slice(scalar_split(s, first, width), first + width))
 
-        def regroup_on_vector(b, t, h):
-            regroup(nc.vector.tensor_copy, b, t, slice(h * N_TILE, scalar_split(b, t, h)))
+        def regroup_on_vector(s, b, t, first, width):
+            regroup(nc.vector.tensor_copy, b, t, slice(first, scalar_split(s, first, width)))
 
-        def quantise(b, t, h):
-            if h == 0:
+        def quantise(b, t, first, width):
+            if first == 0:
                 codes[(b, t)] = mx_pool.tile([P, C], U32, name="codes", align_bytes=64)
                 scales[(b, t)] = mx_pool.tile([P, C], U8, name="scales", align_bytes=64)
-            cols = slice(h * N_TILE, (h + 1) * N_TILE)
+            cols = slice(first, first + width)
             nc.vector.quantize_mx(
                 out=codes[(b, t)][:, cols].bitcast(FP8X4),
                 scales=scales[(b, t)][:, cols],
                 in_=grouped[(b, t)][:, cols, :].rearrange("p c j -> p (c j)"),
             )
 
-        def aggregate(b, t, h):
+        def aggregate(b, t, first, width, vector_helps):
             if t == 0:
                 return
             w = t - 1
-            cols = slice(h * N_TILE, (h + 1) * N_TILE)
+            cols = slice(first, first + width)
             out_rows = out[b, w].rearrange("(p i) c -> p i c", i=M_TILES)
             acc = {}
             for g in range(WIN):
@@ -139,7 +159,7 @@ def tile_stsindividuallayer_pa_t_kernel(tc, data_temb, adj_mid, spatial_emb, out
                     if g == 0:
                         acc[i] = psum.tile([P, N_TILE], F32, name="acc", tag="bank")
                     nc.tensor.matmul_mx(
-                        out=acc[i][:],
+                        out=acc[i][:, :width],
                         lhsT=adj_codes[:, g, i * P : (i + 1) * P].bitcast(FP8X4),
                         lhsT_scale=adj_scales[:, g, i * P : (i + 1) * P],
                         rhs=codes[(b, w + g)][:, cols].bitcast(FP8X4),
@@ -147,29 +167,36 @@ def tile_stsindividuallayer_pa_t_kernel(tc, data_temb, adj_mid, spatial_emb, out
                         start=(g == 0),
                         stop=(g == WIN - 1),
                     )
-            by_halves = w == NW - 1
-            last_chunk = (b, t, h) == chunks[-1]
+            by_tiles = w == NW - 1
             for i in range(M_TILES):
-                if h == 0 and i % 2 == 0:
+                if first == 0 and i % 2 == 0:
                     stage[(b, i // 2)] = stage_pool.tile([P, 2, C], F32, name="stage")
-                empty = nc.vector.tensor_copy if last_chunk and i % 2 == 1 else nc.scalar.copy
-                empty(out=stage[(b, i // 2)][:, i % 2, cols], in_=acc[i][:])
-                if i % 2 == 1 and (by_halves or h == HALVES - 1):
-                    stored = cols if by_halves else slice(0, C)
+                empty = nc.vector.tensor_copy if vector_helps and i % 2 == 1 else nc.scalar.copy
+                empty(out=stage[(b, i // 2)][:, i % 2, cols], in_=acc[i][:, :width])
+                if i % 2 == 1 and (by_tiles or first + width == C):
+                    stored = cols if by_tiles else slice(0, C)
                     nc.sync.dma_start(out=out_rows[:, i - 1 : i + 1, stored], in_=stage[(b, i // 2)][:, :, stored])
 
-        chunks = [(b, t, h) for (b, t) in steps for h in range(HALVES)]
-        for n in range(len(chunks) + 2):
-            if n < len(chunks):
-                add_spatial(*chunks[n])
-            if 1 <= n <= len(chunks):
-                regroup_on_scalar(*chunks[n - 1])
-            if n == ADJ_AT:
+        def finish(n, part):
+            s, b, t, first, width = pieces[n]
+            tiles = [(c, min(N_TILE, first + width - c)) for c in range(first, first + width, N_TILE)]
+            for c, n_cols in tiles[:1] if part == 0 else tiles[1:]:
+                quantise(b, t, c, n_cols)
+                aggregate(b, t, c, n_cols, n >= len(pieces) - VECTOR_HELPS)
+
+        adj_at = [s for s, b, t, first, width in pieces].index(2) + 0
+        for n in range(len(pieces) + 2):
+            if n < len(pieces):
+                add_spatial(*pieces[n])
+            if 1 <= n <= len(pieces):
+                regroup_on_scalar(*pieces[n - 1])
+            if n == adj_at:
                 turn_adj()
-            if n == ADJ_AT + 1:
+            if n == adj_at + 1:
                 quantise_adj()
             if n >= 2:
-                quantise(*chunks[n - 2])
-                aggregate(*chunks[n - 2])
-            if 1 <= n <= len(chunks):
-                regroup_on_vector(*chunks[n - 1])
+                finish(n - 2, 0)
+            if 1 <= n <= len(pieces):
+                regroup_on_vector(*pieces[n - 1])
+            if n >= 2:
+                finish(n - 2, 1)

@@ -14,17 +14,13 @@ NW = T - WIN + 1
 P = 128
 PACK = 4
 N_TILE = 512
+HALVES = C // N_TILE
 M_TILES = NODES // P
 RUN = 8
-FIRST_WIDTHS = (512, 512)
-EARLY_WIDTHS = (512, 512)
-MIDDLE_WIDTHS = (512, 512)
-LAST_WIDTHS = (512, 512)
-EARLY_STEPS = 3
-SCALAR_EARLY = (7, 8)
-SCALAR_BUSY = (3, 16)
-VECTOR_HELPS = 1
-ADJ_AFTER = 2
+SCALAR_COLS_EARLY = 448
+EARLY_HALVES = 6
+SCALAR_COLS_BUSY = 96
+ADJ_AT = 4
 FLOPS = 2 * B * NW * NODES * (WIN * NODES) * C
 
 
@@ -40,20 +36,6 @@ def tile_stsindividuallayer_pa_t_kernel(tc, data_temb, adj_mid, spatial_emb, out
         ctx.enter_context(tc.manual_schedule())
 
         steps = [(b, t) for t in range(T) for b in range(B)]
-        pieces = []
-        for s, (b, t) in enumerate(steps):
-            widths = MIDDLE_WIDTHS
-            if s == 0:
-                widths = FIRST_WIDTHS
-            elif s < EARLY_STEPS:
-                widths = EARLY_WIDTHS
-            elif s == len(steps) - 1:
-                widths = LAST_WIDTHS
-            first = 0
-            for width in widths:
-                pieces.append((s, b, t, first, width))
-                first += width
-
         sp_raw = const.tile([P, PACK, C], BF16)
         adj_raw = const.tile([P, M_TILES, WIN * NODES], BF16)
         raw = {}
@@ -65,17 +47,15 @@ def tile_stsindividuallayer_pa_t_kernel(tc, data_temb, adj_mid, spatial_emb, out
                 out=raw[bt][:], in_=data_temb[bt[0], bt[1]].rearrange("(p j) c -> p j c", j=PACK)
             )
 
-        for s, b, t, first, width in pieces:
-            if s == 0:
-                cols = slice(first, first + width)
-                for tile_, rows in ((sp_raw, spatial_emb[0, 0]), (raw[(b, t)], data_temb[b, t])):
-                    nc.sync.dma_start(
-                        out=tile_[:, :, cols], in_=rows.rearrange("(p j) c -> p j c", j=PACK)[:, :, cols]
-                    )
-        for bt in steps[1:ADJ_AFTER]:
-            load_step(bt)
+        for h in range(HALVES):
+            cols = slice(h * N_TILE, (h + 1) * N_TILE)
+            for tile_, rows in ((sp_raw, spatial_emb[0, 0]), (raw[steps[0]], data_temb[steps[0][0], steps[0][1]])):
+                nc.sync.dma_start(
+                    out=tile_[:, :, cols], in_=rows.rearrange("(p j) c -> p j c", j=PACK)[:, :, cols]
+                )
+        load_step(steps[1])
         nc.sync.dma_start(out=adj_raw[:], in_=adj_mid.rearrange("(p i) k -> p i k", i=M_TILES))
-        for bt in steps[ADJ_AFTER:]:
+        for bt in steps[2:]:
             load_step(bt)
 
         ident = const.tile([P, P], F32)
@@ -109,8 +89,8 @@ def tile_stsindividuallayer_pa_t_kernel(tc, data_temb, adj_mid, spatial_emb, out
 
         grouped, codes, scales, stage = {}, {}, {}, {}
 
-        def add_spatial(s, b, t, first, width):
-            cols = slice(first, first + width)
+        def add_spatial(b, t, h):
+            cols = slice(h * N_TILE, (h + 1) * N_TILE)
             nc.vector.tensor_tensor(
                 out=raw[(b, t)][:, :, cols],
                 in0=raw[(b, t)][:, :, cols],
@@ -124,34 +104,34 @@ def tile_stsindividuallayer_pa_t_kernel(tc, data_temb, adj_mid, spatial_emb, out
                 in_=raw[(b, t)][:, :, cols].rearrange("p j (c r) -> p c j r", r=RUN),
             )
 
-        def scalar_split(s, first, width):
-            share = SCALAR_EARLY if s < EARLY_STEPS else SCALAR_BUSY
-            return first + width - width * share[0] // share[1]
+        def scalar_split(b, t, h):
+            early = halves.index((b, t, h)) < EARLY_HALVES
+            return (h + 1) * N_TILE - (SCALAR_COLS_EARLY if early else SCALAR_COLS_BUSY)
 
-        def regroup_on_scalar(s, b, t, first, width):
-            if first == 0:
+        def regroup_on_scalar(b, t, h):
+            if h == 0:
                 grouped[(b, t)] = grouped_pool.tile([P, C, PACK], BF16, name="grouped", align_bytes=64)
-            regroup(nc.scalar.copy, b, t, slice(scalar_split(s, first, width), first + width))
+            regroup(nc.scalar.copy, b, t, slice(scalar_split(b, t, h), (h + 1) * N_TILE))
 
-        def regroup_on_vector(s, b, t, first, width):
-            regroup(nc.vector.tensor_copy, b, t, slice(first, scalar_split(s, first, width)))
+        def regroup_on_vector(b, t, h):
+            regroup(nc.vector.tensor_copy, b, t, slice(h * N_TILE, scalar_split(b, t, h)))
 
-        def quantise(b, t, first, width):
-            if first == 0:
+        def quantise(b, t, h):
+            if h == 0:
                 codes[(b, t)] = mx_pool.tile([P, C], U32, name="codes", align_bytes=64)
                 scales[(b, t)] = mx_pool.tile([P, C], U8, name="scales", align_bytes=64)
-            cols = slice(first, first + width)
+            cols = slice(h * N_TILE, (h + 1) * N_TILE)
             nc.vector.quantize_mx(
                 out=codes[(b, t)][:, cols].bitcast(FP8X4),
                 scales=scales[(b, t)][:, cols],
                 in_=grouped[(b, t)][:, cols, :].rearrange("p c j -> p (c j)"),
             )
 
-        def aggregate(b, t, first, width, vector_helps):
+        def aggregate(b, t, h):
             if t == 0:
                 return
             w = t - 1
-            cols = slice(first, first + width)
+            cols = slice(h * N_TILE, (h + 1) * N_TILE)
             out_rows = out[b, w].rearrange("(p i) c -> p i c", i=M_TILES)
             acc = {}
             for g in range(WIN):
@@ -159,7 +139,7 @@ def tile_stsindividuallayer_pa_t_kernel(tc, data_temb, adj_mid, spatial_emb, out
                     if g == 0:
                         acc[i] = psum.tile([P, N_TILE], F32, name="acc", tag="bank")
                     nc.tensor.matmul_mx(
-                        out=acc[i][:, :width],
+                        out=acc[i][:],
                         lhsT=adj_codes[:, g, i * P : (i + 1) * P].bitcast(FP8X4),
                         lhsT_scale=adj_scales[:, g, i * P : (i + 1) * P],
                         rhs=codes[(b, w + g)][:, cols].bitcast(FP8X4),
@@ -167,36 +147,29 @@ def tile_stsindividuallayer_pa_t_kernel(tc, data_temb, adj_mid, spatial_emb, out
                         start=(g == 0),
                         stop=(g == WIN - 1),
                     )
-            by_tiles = w == NW - 1
+            by_halves = w >= NW - 2
+            last_half = (b, t, h) == halves[-1]
             for i in range(M_TILES):
-                if first == 0 and i % 2 == 0:
+                if h == 0 and i % 2 == 0:
                     stage[(b, i // 2)] = stage_pool.tile([P, 2, C], F32, name="stage")
-                empty = nc.vector.tensor_copy if vector_helps and i % 2 == 1 else nc.scalar.copy
-                empty(out=stage[(b, i // 2)][:, i % 2, cols], in_=acc[i][:, :width])
-                if i % 2 == 1 and (by_tiles or first + width == C):
-                    stored = cols if by_tiles else slice(0, C)
+                empty = nc.vector.tensor_copy if last_half and i % 2 == 1 else nc.scalar.copy
+                empty(out=stage[(b, i // 2)][:, i % 2, cols], in_=acc[i][:])
+                if i % 2 == 1 and (by_halves or h == HALVES - 1):
+                    stored = cols if by_halves else slice(0, C)
                     nc.sync.dma_start(out=out_rows[:, i - 1 : i + 1, stored], in_=stage[(b, i // 2)][:, :, stored])
 
-        def finish(n, part):
-            s, b, t, first, width = pieces[n]
-            tiles = [(c, min(N_TILE, first + width - c)) for c in range(first, first + width, N_TILE)]
-            for c, n_cols in tiles[:1] if part == 0 else tiles[1:]:
-                quantise(b, t, c, n_cols)
-                aggregate(b, t, c, n_cols, n >= len(pieces) - VECTOR_HELPS)
-
-        adj_at = [s for s, b, t, first, width in pieces].index(2) + 0
-        for n in range(len(pieces) + 2):
-            if n < len(pieces):
-                add_spatial(*pieces[n])
-            if 1 <= n <= len(pieces):
-                regroup_on_scalar(*pieces[n - 1])
-            if n == adj_at:
+        halves = [(b, t, h) for (b, t) in steps for h in range(HALVES)]
+        for n in range(len(halves) + 2):
+            if n < len(halves):
+                add_spatial(*halves[n])
+            if 1 <= n <= len(halves):
+                regroup_on_scalar(*halves[n - 1])
+            if n == ADJ_AT:
                 turn_adj()
-            if n == adj_at + 1:
+            if n == ADJ_AT + 1:
                 quantise_adj()
             if n >= 2:
-                finish(n - 2, 0)
-            if 1 <= n <= len(pieces):
-                regroup_on_vector(*pieces[n - 1])
-            if n >= 2:
-                finish(n - 2, 1)
+                quantise(*halves[n - 2])
+                aggregate(*halves[n - 2])
+            if 1 <= n <= len(halves):
+                regroup_on_vector(*halves[n - 1])

from contextlib import ExitStack

import concourse.mybir as mybir
from concourse.masks import make_identity

F32 = mybir.dt.float32
BF16 = mybir.dt.bfloat16
U32 = mybir.dt.uint32
U8 = mybir.dt.uint8
FP8X4 = mybir.dt.float8_e4m3fn_x4

B, T, NODES, C, WIN = 2, 5, 512, 1024, 2
NW = T - WIN + 1
P = 128
PACK = 4
N_TILE = 512
HALVES = C // N_TILE
M_TILES = NODES // P
RUN = 8
SCALAR_COLS_EARLY = 448
EARLY_HALVES = 6
SCALAR_COLS_BUSY = 96
ADJ_AT = 4
FLOPS = 2 * B * NW * NODES * (WIN * NODES) * C


def tile_stsindividuallayer_pa_t_kernel(tc, data_temb, adj_mid, spatial_emb, out):
    nc = tc.nc
    with ExitStack() as ctx:
        const = ctx.enter_context(tc.tile_pool(name="const", bufs=1))
        raw_pool = ctx.enter_context(tc.tile_pool(name="raw", bufs=B * T))
        grouped_pool = ctx.enter_context(tc.tile_pool(name="grouped", bufs=3))
        mx_pool = ctx.enter_context(tc.tile_pool(name="mx", bufs=6))
        stage_pool = ctx.enter_context(tc.tile_pool(name="stage", bufs=8))
        psum = ctx.enter_context(tc.psum_pool(name="psum", bufs=8))
        ctx.enter_context(tc.manual_schedule())

        steps = [(b, t) for t in range(T) for b in range(B)]
        sp_raw = const.tile([P, PACK, C], BF16)
        adj_raw = const.tile([P, M_TILES, WIN * NODES], BF16)
        raw = {}
        for bt in steps:
            raw[bt] = raw_pool.tile([P, PACK, C], BF16, name="raw")

        def load_step(bt):
            nc.sync.dma_start(
                out=raw[bt][:], in_=data_temb[bt[0], bt[1]].rearrange("(p j) c -> p j c", j=PACK)
            )

        for h in range(HALVES):
            cols = slice(h * N_TILE, (h + 1) * N_TILE)
            for tile_, rows in ((sp_raw, spatial_emb[0, 0]), (raw[steps[0]], data_temb[steps[0][0], steps[0][1]])):
                nc.sync.dma_start(
                    out=tile_[:, :, cols], in_=rows.rearrange("(p j) c -> p j c", j=PACK)[:, :, cols]
                )
        load_step(steps[1])
        nc.sync.dma_start(out=adj_raw[:], in_=adj_mid.rearrange("(p i) k -> p i k", i=M_TILES))
        for bt in steps[2:]:
            load_step(bt)

        ident = const.tile([P, P], F32)
        make_identity(nc, ident[:])

        adj_words = adj_raw[:].bitcast(F32).rearrange("p i (g q u) -> p i g q u", g=WIN, u=2)
        adj_grouped = const.tile([P, WIN, M_TILES * P * PACK], BF16, align_bytes=64)
        adj_grouped_words = adj_grouped[:].bitcast(F32).rearrange(
            "p g (i m u) -> p g i m u", i=M_TILES, u=2
        )
        adj_codes = const.tile([P, WIN, NODES], U32, align_bytes=64)
        adj_scales = const.tile([P, WIN, NODES], U8, align_bytes=64)

        def turn_adj():
            for g in range(WIN):
                for i0 in range(0, M_TILES, 2):
                    turned = psum.tile([P, 2, 2, P], F32, tag="bank")
                    for i in range(2):
                        for u in range(2):
                            nc.tensor.transpose(turned[:, i, u, :], adj_words[:, i0 + i, g, :, u], ident[:])
                    nc.scalar.copy(
                        out=adj_grouped_words[:, g, i0 : i0 + 2, :, :],
                        in_=turned[:].rearrange("p i u m -> p i m u"),
                    )

        def quantise_adj():
            for g in range(WIN):
                nc.vector.quantize_mx(
                    out=adj_codes[:, g, :].bitcast(FP8X4), scales=adj_scales[:, g, :], in_=adj_grouped[:, g, :]
                )

        grouped, codes, scales, stage = {}, {}, {}, {}

        def add_spatial(b, t, h):
            cols = slice(h * N_TILE, (h + 1) * N_TILE)
            nc.vector.tensor_tensor(
                out=raw[(b, t)][:, :, cols],
                in0=raw[(b, t)][:, :, cols],
                in1=sp_raw[:, :, cols],
                op=mybir.AluOpType.add,
            )

        def regroup(copy, b, t, cols):
            copy(
                out=grouped[(b, t)][:, cols, :].rearrange("p (c r) j -> p c j r", r=RUN),
                in_=raw[(b, t)][:, :, cols].rearrange("p j (c r) -> p c j r", r=RUN),
            )

        def scalar_split(b, t, h):
            early = halves.index((b, t, h)) < EARLY_HALVES
            return (h + 1) * N_TILE - (SCALAR_COLS_EARLY if early else SCALAR_COLS_BUSY)

        def regroup_on_scalar(b, t, h):
            if h == 0:
                grouped[(b, t)] = grouped_pool.tile([P, C, PACK], BF16, name="grouped", align_bytes=64)
            regroup(nc.scalar.copy, b, t, slice(scalar_split(b, t, h), (h + 1) * N_TILE))

        def regroup_on_vector(b, t, h):
            regroup(nc.vector.tensor_copy, b, t, slice(h * N_TILE, scalar_split(b, t, h)))

        def quantise(b, t, h):
            if h == 0:
                codes[(b, t)] = mx_pool.tile([P, C], U32, name="codes", align_bytes=64)
                scales[(b, t)] = mx_pool.tile([P, C], U8, name="scales", align_bytes=64)
            cols = slice(h * N_TILE, (h + 1) * N_TILE)
            nc.vector.quantize_mx(
                out=codes[(b, t)][:, cols].bitcast(FP8X4),
                scales=scales[(b, t)][:, cols],
                in_=grouped[(b, t)][:, cols, :].rearrange("p c j -> p (c j)"),
            )

        def aggregate(b, t, h):
            if t == 0:
                return
            w = t - 1
            cols = slice(h * N_TILE, (h + 1) * N_TILE)
            out_rows = out[b, w].rearrange("(p i) c -> p i c", i=M_TILES)
            acc = {}
            for g in range(WIN):
                for i in range(M_TILES):
                    if g == 0:
                        acc[i] = psum.tile([P, N_TILE], F32, name="acc", tag="bank")
                    nc.tensor.matmul_mx(
                        out=acc[i][:],
                        lhsT=adj_codes[:, g, i * P : (i + 1) * P].bitcast(FP8X4),
                        lhsT_scale=adj_scales[:, g, i * P : (i + 1) * P],
                        rhs=codes[(b, w + g)][:, cols].bitcast(FP8X4),
                        rhs_scale=scales[(b, w + g)][:, cols],
                        start=(g == 0),
                        stop=(g == WIN - 1),
                    )
            by_halves = w >= NW - 2
            last_half = (b, t, h) == halves[-1]
            for i in range(M_TILES):
                if h == 0 and i % 2 == 0:
                    stage[(b, i // 2)] = stage_pool.tile([P, 2, C], F32, name="stage")
                empty = nc.vector.tensor_copy if last_half and i % 2 == 1 else nc.scalar.copy
                empty(out=stage[(b, i // 2)][:, i % 2, cols], in_=acc[i][:])
                if i % 2 == 1 and (by_halves or h == HALVES - 1):
                    stored = cols if by_halves else slice(0, C)
                    nc.sync.dma_start(out=out_rows[:, i - 1 : i + 1, stored], in_=stage[(b, i // 2)][:, :, stored])

        halves = [(b, t, h) for (b, t) in steps for h in range(HALVES)]
        for n in range(len(halves) + 2):
            if n < len(halves):
                add_spatial(*halves[n])
            if 1 <= n <= len(halves):
                regroup_on_scalar(*halves[n - 1])
            if n == ADJ_AT:
                turn_adj()
            if n == ADJ_AT + 1:
                quantise_adj()
            if n >= 2:
                quantise(*halves[n - 2])
                aggregate(*halves[n - 2])
            if 1 <= n <= len(halves):
                regroup_on_vector(*halves[n - 1])
